import numpy as np
import ml_dtypes


def mxq(x, axis, fmt="e4m3"):
    dtype, down = {"e4m3": (ml_dtypes.float8_e4m3fn, 7), "e5m2": (ml_dtypes.float8_e5m2, 14)}[fmt]
    v = np.moveaxis(np.asarray(x, np.float32).astype(ml_dtypes.bfloat16).astype(np.float64), axis, -1)
    blocks = v.reshape(v.shape[:-1] + (-1, 32))
    amax = np.abs(blocks).max(-1, keepdims=True)
    byte = np.maximum(np.where(amax > 0, np.frexp(amax)[1] - 1 + 127, 0) - down, 1)
    scale = np.exp2(byte - 127.0)
    codes = (blocks / scale).astype(np.float32).astype(dtype).astype(np.float64)
    return np.moveaxis((codes * scale).reshape(v.shape), -1, axis)


WIDE = False


def mx_kscale(k):
    if not WIDE:
        return np.ones(k)
    levels = np.array([30, -30])
    if k % 512:
        return np.exp2(np.random.permutation(np.resize(levels, k // 32))).repeat(32)
    a = np.empty((k // 512, 16))
    for p in range(k // 512):
        a[p, :8] = np.random.permutation(np.resize(levels, 8))
        for g in range(8):
            far = levels[np.abs(levels - a[p, g]) >= 10]
            a[p, g + 8] = far[np.random.randint(len(far))]
    return np.exp2(a.ravel()).repeat(32)


BF16 = ml_dtypes.bfloat16


def bf(x):
    return np.asarray(x, np.float32).astype(BF16)


def f64(x):
    return np.asarray(x).astype(np.float64)


B, S, H, NH, DH, G = 1, 512, 2048, 16, 128, 4
NKV = NH // G
ROPE_THETA = 10000.0


def rope(x):
    inv_freq = 1.0 / ROPE_THETA ** (np.arange(0, DH, 2) / DH)
    angles = np.arange(S)[:, None] * inv_freq[None, :]
    cos = np.cos(angles)[None, :, None, :]
    sin = np.sin(angles)[None, :, None, :]
    x1, x2 = np.split(x, 2, axis=-1)
    return np.concatenate([x1 * cos - x2 * sin, x1 * sin + x2 * cos], axis=-1)


def setup_inputs():
    s = mx_kscale(H)
    return {
        "hidden_states": bf(np.random.standard_normal((B, S, H)) * s),
        "Wq": bf(np.random.standard_normal((H, NH * DH)) * 1.4 / np.sqrt(H) / s[:, None]),
        "bq": bf(np.random.standard_normal(NH * DH) * 0.2),
        "Wk": bf(np.random.standard_normal((H, NKV * DH)) * 1.4 / np.sqrt(H) / s[:, None]),
        "bk": bf(np.random.standard_normal(NKV * DH) * 0.2),
        "Wv": bf(np.random.standard_normal((H, NKV * DH)) / np.sqrt(H) / s[:, None]),
        "bv": bf(np.random.standard_normal(NKV * DH) * 0.2),
    }


def reference(hidden_states, Wq, bq, Wk, bk, Wv, bv):
    xq = mxq(f64(hidden_states), 2, "e5m2")
    q = ((xq @ mxq(f64(Wq), 0, "e5m2")) + f64(bq)).reshape(B, S, NH, DH)
    k = ((xq @ mxq(f64(Wk), 0, "e5m2")) + f64(bk)).reshape(B, S, NKV, DH)
    v = ((xq @ mxq(f64(Wv), 0, "e5m2")) + f64(bv)).reshape(B, S, NKV, DH)
    q = rope(q)
    k = rope(k)
    return q.transpose(0, 2, 1, 3), k.transpose(0, 2, 1, 3), v.transpose(0, 2, 1, 3)

@@ -1,0 +1,347 @@
+from contextlib import ExitStack
+
+import concourse.mybir as mybir
+from concourse.masks import make_identity
+
+S_LEN, H, NH, NKV, DH = 512, 2048, 16, 4, 128
+FLOPS = 2 * S_LEN * H * (NH + 2 * NKV) * DH
+
+F32 = mybir.dt.float32
+BF16 = mybir.dt.bfloat16
+U32 = mybir.dt.uint32
+U8 = mybir.dt.uint8
+I32 = mybir.dt.int32
+E5 = mybir.dt.float8_e5m2_x4
+ALU = mybir.AluOpType
+ACT = mybir.ActivationFunctionType
+
+P = 128
+PACK = 4
+K_PASS = P * PACK
+G = H // K_PASS
+NT = S_LEN // P
+CH = 512
+NCHUNK = 6
+
+PI = 3.141592653589793
+C1 = 6.28125
+C2 = 2.0 * PI - C1
+MAGIC = 12582912.0
+THETA = 10000.0
+
+USE_G = True
+GCOLS = 64
+FAST = False
+
+
+def tile_autoreggqaattention_pa_kernel(tc, hidden_states, Wq, bq, Wk, bk, Wv, bv, out_0, out_1, out_2):
+    nc = tc.nc
+    with ExitStack() as ctx:
+        const = ctx.enter_context(tc.tile_pool(name="const", bufs=1))
+        tmp = ctx.enter_context(tc.tile_pool(name="tmp", bufs=4))
+        rawp = ctx.enter_context(tc.tile_pool(name="rawp", bufs=5))
+        gpool = ctx.enter_context(tc.tile_pool(name="gpool", bufs=1))
+        cpool = ctx.enter_context(tc.tile_pool(name="cpool", bufs=8))
+        apool = ctx.enter_context(tc.tile_pool(name="apool", bufs=4))
+        opool = ctx.enter_context(tc.tile_pool(name="opool", bufs=4))
+        psa = ctx.enter_context(tc.psum_pool(name="psa", bufs=4))
+        psb = ctx.enter_context(tc.psum_pool(name="psb", bufs=4))
+        ctx.enter_context(tc.manual_schedule())
+
+        def w_rows(c, g):
+            rows = slice(g * K_PASS, (g + 1) * K_PASS)
+            if c == 0:
+                src = Wk[rows, :]
+            elif c == NCHUNK - 1:
+                src = Wv[rows, :]
+            else:
+                src = Wq[rows, (c - 1) * CH:c * CH]
+            return src.rearrange("(p j) w -> p j w", j=PACK)
+
+        raw = {}
+
+        def alloc_raw(c):
+            raw[c] = rawp.tile([P, G, PACK, CH], BF16, tag="raw", name="raw%d" % c)
+
+        def load_w(c, g):
+            nc.sync.dma_start(out=raw[c][:, g, :, :], in_=w_rows(c, g))
+
+        brow = const.tile([P, P], BF16, name="brow")
+        nc.gpsimd.memset(brow[:], 0.0)
+        nc.scalar.dma_start(out=brow[0:NH, :], in_=bq.rearrange("(h d) -> h d", d=DH))
+        nc.scalar.dma_start(out=brow[NH:NH + NKV, :], in_=bk.rearrange("(h d) -> h d", d=DH))
+        nc.scalar.dma_start(out=brow[NH + NKV:NH + 2 * NKV, :], in_=bv.rearrange("(h d) -> h d", d=DH))
+
+        x_sb = const.tile([P, NT, H], BF16, name="x_sb")
+        xv = hidden_states.rearrange("b (p t) k -> p (b t) k", t=NT)
+        alloc_raw(0)
+        load_w(0, 0)
+        load_w(0, 1)
+        for t in range(NT):
+            nc.sync.dma_start(out=x_sb[:, t, :], in_=xv[:, t, :])
+        load_w(0, 2)
+        load_w(0, 3)
+        for c in range(1, NCHUNK - 1):
+            alloc_raw(c)
+            for g in range(G):
+                load_w(c, g)
+
+        zero1 = const.tile([P, 1], F32, name="zero1")
+        nc.gpsimd.memset(zero1[:], 0.0)
+        warm = const.tile([P, 1], F32, name="warm")
+        nc.scalar.activation(out=warm[:], in_=zero1[:], func=ACT.Sin)
+
+        idxn = const.tile([P, 8], I32, name="idxn")
+        nc.gpsimd.iota(idxn[:], pattern=[[0, 8]], base=P - 1, channel_multiplier=-1)
+        colj = const.tile([P, 8], I32, name="colj")
+        nc.gpsimd.iota(colj[:], pattern=[[1, 8]], base=0, channel_multiplier=0)
+        pos = tmp.tile([P, S_LEN], F32, tag="t", name="pos")
+        nc.gpsimd.iota(pos[:], pattern=[[1, NT], [NT, P]], base=0, channel_multiplier=0, allow_small_or_imprecise_dtypes=True)
+        ident = const.tile([P, P], F32, name="ident")
+        make_identity(nc, ident[:])
+        pswap = const.tile([P, P], F32, name="pswap")
+        nc.gpsimd.tensor_copy(out=pswap[:, 0:64], in_=ident[:, 64:128])
+        nc.gpsimd.tensor_copy(out=pswap[:, 64:128], in_=ident[:, 0:64])
+
+        shf = const.tile([P, 8], I32, name="shf")
+        nc.vector.tensor_tensor(out=shf[:], in0=idxn[:], in1=colj[:], op=ALU.logical_shift_right)
+        nbit = const.tile([P, 8], I32, name="nbit")
+        nc.vector.tensor_single_scalar(out=nbit[:], in_=shf[:], scalar=1, op=ALU.bitwise_and)
+        fac = const.tile([P, 8], F32, name="fac")
+        for j in range(6):
+            gj = THETA ** (-(2.0 ** j) / 64.0)
+            nc.vector.tensor_scalar(out=fac[:, j:j + 1], in0=nbit[:, j:j + 1], scalar1=1.0 - gj, scalar2=gj, op0=ALU.mult, op1=ALU.add)
+        sgn2 = const.tile([P, 1], F32, name="sgn2")
+        nc.vector.tensor_scalar(out=sgn2[:], in0=nbit[:, 6:7], scalar1=4.0, scalar2=-2.0, op0=ALU.mult, op1=ALU.add)
+        halfpi = const.tile([P, 1], F32, name="halfpi")
+        nc.vector.tensor_scalar(out=halfpi[:], in0=nbit[:, 6:7], scalar1=0.0, scalar2=PI / 2.0, op0=ALU.mult, op1=ALU.add)
+        pr3 = const.tile([P, 4], F32, name="pr3")
+        nc.vector.tensor_tensor(out=pr3[:, 0:3], in0=fac[:, 0:3], in1=fac[:, 3:6], op=ALU.mult)
+        wfr = const.tile([P, 4], F32, name="wfr")
+        nc.vector.tensor_tensor(out=wfr[:, 0:1], in0=pr3[:, 0:1], in1=pr3[:, 1:2], op=ALU.mult)
+        nc.vector.tensor_tensor(out=wfr[:, 1:2], in0=wfr[:, 0:1], in1=pr3[:, 2:3], op=ALU.mult)
+        nc.vector.tensor_scalar(out=wfr[:, 2:3], in0=wfr[:, 1:2], scalar1=1.0 / (2.0 * PI), scalar2=None, op0=ALU.mult)
+
+        ang = tmp.tile([P, S_LEN], F32, tag="t", name="ang")
+        nc.vector.tensor_scalar(out=ang[:], in0=pos[:], scalar1=wfr[:, 1:2], scalar2=None, op0=ALU.mult)
+        turns = tmp.tile([P, S_LEN], F32, tag="t", name="turns")
+        nc.vector.tensor_scalar(out=turns[:], in0=pos[:], scalar1=wfr[:, 2:3], scalar2=MAGIC, op0=ALU.mult, op1=ALU.add)
+        nint = tmp.tile([P, S_LEN], I32, tag="t", name="nint")
+        nc.vector.tensor_scalar(out=nint[:], in0=turns[:], scalar1=-MAGIC, scalar2=None, op0=ALU.add)
+        nc.vector.scalar_tensor_tensor(out=ang[:], in0=nint[:], scalar=-C1, in1=ang[:], op0=ALU.mult, op1=ALU.add)
+        nc.vector.scalar_tensor_tensor(out=ang[:], in0=nint[:], scalar=-C2, in1=ang[:], op0=ALU.mult, op1=ALU.add)
+        mab = tmp.tile([P, S_LEN], F32, tag="t", name="mab")
+        nc.vector.scalar_tensor_tensor(out=mab[:], in0=ang[:], scalar=-1.0, in1=ang[:], op0=ALU.mult, op1=ALU.min)
+
+        def copy_on(eng, out, in_):
+            if eng == "V":
+                nc.vector.tensor_copy(out=out, in_=in_)
+            elif eng == "S":
+                nc.scalar.copy(out=out, in_=in_)
+            else:
+                nc.gpsimd.tensor_scalar(out=out, in0=in_, scalar1=1.0, scalar2=0.0, op0=ALU.mult, op1=ALU.add)
+
+        def grp_tile(tag, bufs, shape):
+            return gpool.tile(shape, BF16, tag=tag, name=tag, bufs=bufs, align_bytes=64)
+
+        def ilv_pass(eng, grp, g):
+            copy_on(eng, grp[:], raw[0][:, g, :, :].rearrange("p j w -> p w j"))
+
+        def ilv_head(eng, grp, c, hh, w0, w1):
+            src = raw[c][:, :, :, hh * DH + w0:hh * DH + w1]
+            dst = grp[:, :, w0:w1, :]
+            if FAST:
+                for g in range(G):
+                    copy_on(eng, dst[:, g, :, :].rearrange("p (c i) j -> p c j i", i=4), src[:, g, :, :].rearrange("p j (c i) -> p c j i", i=4))
+            else:
+                copy_on(eng, dst, src.rearrange("p g j w -> p g w j"))
+
+        def quant(grp_flat):
+            wc = cpool.tile([P, CH], U32, tag="wc", name="wc", align_bytes=64)
+            ws = cpool.tile([P, CH], U8, tag="ws", name="ws", align_bytes=64)
+            nc.vector.quantize_mx(out=wc[:].bitcast(E5), scales=ws[:], in_=grp_flat)
+            return wc, ws
+
+        codes = {}
+        g0 = grp_tile("gs", 3, [P, CH, PACK])
+        ilv_pass("S", g0, 0)
+        browf = const.tile([P, P], F32, name="browf")
+        nc.vector.tensor_copy(out=browf[:], in_=brow[:])
+        bps = psb.tile([P, P], F32, tag="tr", name="bps")
+        nc.tensor.transpose(bps[:], browf[:], ident[:])
+        g1 = grp_tile("gm", 1, [P, CH, PACK])
+        ilv_pass("V", g1, 1)
+
+        sinh_ = tmp.tile([P, S_LEN], F32, tag="t", name="sinh_")
+        nc.scalar.activation(out=sinh_[:], in_=ang[:], func=ACT.Sin, scale=0.5)
+        cosh_ = tmp.tile([P, S_LEN], F32, tag="t", name="cosh_")
+        nc.scalar.activation(out=cosh_[:], in_=mab[:], func=ACT.Sin, bias=halfpi[:, 0:1], scale=0.5)
+        cos_t = const.tile([P, S_LEN], F32, name="cos_t")
+        nc.scalar.activation(out=cos_t[:], in_=mab[:], func=ACT.Sin, bias=halfpi[:, 0:1], scale=1.0)
+
+        codes[(0, 0)] = quant(g0[:].rearrange("p w j -> p (w j)"))
+        codes[(0, 1)] = quant(g1[:].rearrange("p w j -> p (w j)"))
+        bias = const.tile([P, 32], F32, name="bias")
+        nc.vector.tensor_copy(out=bias[:, 0:NH + 2 * NKV], in_=bps[:, 0:NH + 2 * NKV])
+        sin_t = const.tile([P, S_LEN], F32, name="sin_t")
+        nc.vector.scalar_tensor_tensor(out=sin_t[:], in0=sinh_[:], scalar=sgn2[:, 0:1], in1=cosh_[:], op0=ALU.mult, op1=ALU.mult)
+
+        xw = x_sb[:].bitcast(F32)
+        xg = const.tile([P, G, S_LEN * PACK], BF16, name="xg", align_bytes=64)
+        xgw = xg[:].bitcast(F32).rearrange("p g (r u) -> p g r u", u=2)
+        xc = const.tile([P, G, S_LEN], U32, name="xc", align_bytes=64)
+        xs = const.tile([P, G, S_LEN], U8, name="xs", align_bytes=64)
+
+        def x_tile(t, engs):
+            for gp in range(2):
+                bank = psb.tile([P, 2, 2, P], F32, tag="tr", name="xbank")
+                for g2 in range(2):
+                    w0 = 256 * (2 * gp + g2)
+                    for u in range(2):
+                        nc.tensor.transpose(bank[:, g2, u, :], xw[:, t, w0 + u:w0 + 256:2], ident[:])
+                dst = xgw[:, 2 * gp:2 * gp + 2, t * P:(t + 1) * P, :]
+                src = bank[:].rearrange("p g u r -> p g r u")
+                if engs[gp] == "S":
+                    nc.scalar.copy(out=dst, in_=src)
+                else:
+                    nc.vector.tensor_copy(out=dst, in_=src)
+
+        def x_quant(tp):
+            for g in range(G):
+                nc.vector.quantize_mx(
+                    out=xc[:, g, tp * 256:(tp + 1) * 256].bitcast(E5),
+                    scales=xs[:, g, tp * 256:(tp + 1) * 256],
+                    in_=xg[:, g, tp * 1024:(tp + 1) * 1024],
+                )
+
+        x_tile(0, "SS")
+        x_tile(1, "SV")
+        x_quant(0)
+        x_tile(2, "SV")
+        x_tile(3, "SV")
+        g2t = grp_tile("gs", 3, [P, CH, PACK])
+        ilv_pass("S", g2t, 2)
+        x_quant(1)
+        g3t = grp_tile("gg", 1, [P, CH, PACK])
+        ilv_pass("V", g3t, 3)
+        codes[(0, 2)] = quant(g2t[:].rearrange("p w j -> p (w j)"))
+        codes[(0, 3)] = quant(g3t[:].rearrange("p w j -> p (w j)"))
+
+        acc = {}
+        prod = {}
+        trb = {}
+
+        def mx(c, hh):
+            a = psa.tile([P, S_LEN], F32, tag="acc", name="acc")
+            acc[(c, hh)] = a
+            for g in range(G):
+                if c == 0:
+                    wc, ws = codes[(0, g)]
+                    cols = slice(hh * DH, (hh + 1) * DH)
+                else:
+                    wc, ws = codes[(c, hh)]
+                    cols = slice(g * DH, (g + 1) * DH)
+                nc.tensor.matmul_mx(
+                    out=a[:],
+                    lhsT=wc[:, cols].bitcast(E5),
+                    lhsT_scale=ws[:, cols],
+                    rhs=xc[:, g, :].bitcast(E5),
+                    rhs_scale=xs[:, g, :],
+                    start=(g == 0),
+                    stop=(g == G - 1),
+                )
+
+        def bias_col(c, hh):
+            if c == 0:
+                k = NH + hh
+            elif c == NCHUNK - 1:
+                k = NH + NKV + hh
+            else:
+                k = (c - 1) * 4 + hh
+            return bias[:, k:k + 1]
+
+        def products(c, hh):
+            a = acc[(c, hh)]
+            ta = apool.tile([P, S_LEN], F32, tag="ta", name="ta")
+            if c == NCHUNK - 1:
+                nc.vector.tensor_scalar(out=ta[:], in0=a[:], scalar1=bias_col(c, hh), scalar2=None, op0=ALU.add)
+                prod[(c, hh)] = (ta,)
+            else:
+                tb = apool.tile([P, S_LEN], F32, tag="tb", name="tb")
+                nc.vector.scalar_tensor_tensor(out=ta[:], in0=a[:], scalar=bias_col(c, hh), in1=cos_t[:], op0=ALU.add, op1=ALU.mult)
+                nc.vector.scalar_tensor_tensor(out=tb[:], in0=a[:], scalar=bias_col(c, hh), in1=sin_t[:], op0=ALU.add, op1=ALU.mult)
+                prod[(c, hh)] = (ta, tb)
+
+        def turn(c, hh):
+            tr = psb.tile([P, S_LEN], F32, tag="tr", name="tr")
+            trb[(c, hh)] = tr
+            pr = prod[(c, hh)]
+            for t in range(NT):
+                blk = slice(t * P, (t + 1) * P)
+                if len(pr) == 1:
+                    nc.tensor.transpose(tr[:, blk], pr[0][:, blk], ident[:])
+                else:
+                    nc.tensor.matmul(out=tr[:, blk], lhsT=pr[0][:, blk], rhs=ident[:], is_transpose=True, start=True, stop=False)
+                    nc.tensor.matmul(out=tr[:, blk], lhsT=pr[1][:, blk], rhs=pswap[:], is_transpose=True, start=False, stop=True)
+
+        def leave(c, hh):
+            if c == 0:
+                dst = out_1[0, hh]
+            elif c == NCHUNK - 1:
+                dst = out_2[0, hh]
+            else:
+                dst = out_0[0, (c - 1) * 4 + hh]
+            o = opool.tile([P, S_LEN], F32, tag="o", name="o")
+            nc.scalar.copy(out=o[:], in_=trb[(c, hh)][:])
+            nc.scalar.dma_start(out=dst.rearrange("(p t) d -> p (t d)", t=NT), in_=o[:])
+
+        for hh in range(4):
+            mx(0, hh)
+
+        HS = [P, G, DH, PACK]
+        for c in range(NCHUNK - 1):
+            nx = c + 1
+            if c == 0:
+                alloc_raw(NCHUNK - 1)
+                for g in range(G):
+                    load_w(NCHUNK - 1, g)
+            u0 = grp_tile("gs", 3, HS)
+            ilv_head("S", u0, nx, 0, 0, DH)
+            u1 = grp_tile("gs", 3, HS)
+            ilv_head("S", u1, nx, 1, 0, DH)
+            u3 = grp_tile("gg", 1, HS)
+            u2 = grp_tile("gm", 1, HS)
+            if USE_G:
+                ilv_head("G", u3, nx, 3, 0, DH)
+                ilv_head("G", u2, nx, 2, 0, GCOLS)
+            for hh in range(4):
+                products(c, hh)
+            if USE_G:
+                ilv_head("V", u2, nx, 2, GCOLS, DH)
+            else:
+                ilv_head("V", u2, nx, 2, 0, DH)
+            flat = "p g w j -> p (g w j)"
+            codes[(nx, 0)] = quant(u0[:].rearrange(flat))
+            codes[(nx, 1)] = quant(u1[:].rearrange(flat))
+            if not USE_G:
+                ilv_head("V", u3, nx, 3, 0, 32)
+                ilv_head("S", u3, nx, 3, 32, DH)
+            codes[(nx, 2)] = quant(u2[:].rearrange(flat))
+            codes[(nx, 3)] = quant(u3[:].rearrange(flat))
+            for hh in range(4):
+                turn(c, hh)
+            if nx < NCHUNK - 1:
+                for hh in range(4):
+                    mx(nx, hh)
+            for hh in range(4):
+                leave(c, hh)
+
+        c = NCHUNK - 1
+        mx(c, 0)
+        mx(c, 1)
+        for hh in range(4):
+            products(c, hh)
+            turn(c, hh)
+            leave(c, hh)
+            if hh + 2 < 4:
+                mx(c, hh + 2)

@@ -29,7 +29,7 @@ C2 = 2.0 * PI - C1
 MAGIC = 12582912.0
 THETA = 10000.0
 
-USE_G = True
+USE_G = False
 GCOLS = 64
 FAST = False
 

@@ -24,14 +24,13 @@ CH = 512
 NCHUNK = 6
 
 PI = 3.141592653589793
-C1 = 6.28125
-C2 = 2.0 * PI - C1
 MAGIC = 12582912.0
 THETA = 10000.0
 
-USE_G = False
-GCOLS = 64
-FAST = False
+GCOLS = 96
+SCOLS = 32
+FAST = ''
+PRELOAD = 3
 
 
 def tile_autoreggqaattention_pa_kernel(tc, hidden_states, Wq, bq, Wk, bk, Wv, bv, out_0, out_1, out_2):
@@ -39,9 +38,9 @@ def tile_autoreggqaattention_pa_kernel(tc, hidden_states, Wq, bq, Wk, bk, Wv, bv
     with ExitStack() as ctx:
         const = ctx.enter_context(tc.tile_pool(name="const", bufs=1))
         tmp = ctx.enter_context(tc.tile_pool(name="tmp", bufs=4))
-        rawp = ctx.enter_context(tc.tile_pool(name="rawp", bufs=5))
+        rawp = ctx.enter_context(tc.tile_pool(name="rawp", bufs=4))
         gpool = ctx.enter_context(tc.tile_pool(name="gpool", bufs=1))
-        cpool = ctx.enter_context(tc.tile_pool(name="cpool", bufs=8))
+        cpool = ctx.enter_context(tc.tile_pool(name="cpool", bufs=4))
         apool = ctx.enter_context(tc.tile_pool(name="apool", bufs=4))
         opool = ctx.enter_context(tc.tile_pool(name="opool", bufs=4))
         psa = ctx.enter_context(tc.psum_pool(name="psa", bufs=4))
@@ -81,7 +80,7 @@ def tile_autoreggqaattention_pa_kernel(tc, hidden_states, Wq, bq, Wk, bk, Wv, bv
             nc.sync.dma_start(out=x_sb[:, t, :], in_=xv[:, t, :])
         load_w(0, 2)
         load_w(0, 3)
-        for c in range(1, NCHUNK - 1):
+        for c in range(1, PRELOAD):
             alloc_raw(c)
             for g in range(G):
                 load_w(c, g)
@@ -123,13 +122,12 @@ def tile_autoreggqaattention_pa_kernel(tc, hidden_states, Wq, bq, Wk, bk, Wv, bv
         nc.vector.tensor_scalar(out=wfr[:, 2:3], in0=wfr[:, 1:2], scalar1=1.0 / (2.0 * PI), scalar2=None, op0=ALU.mult)
 
         ang = tmp.tile([P, S_LEN], F32, tag="t", name="ang")
-        nc.vector.tensor_scalar(out=ang[:], in0=pos[:], scalar1=wfr[:, 1:2], scalar2=None, op0=ALU.mult)
+        nc.scalar.activation(out=ang[:], in_=pos[:], func=ACT.Identity, scale=wfr[:, 1:2])
         turns = tmp.tile([P, S_LEN], F32, tag="t", name="turns")
         nc.vector.tensor_scalar(out=turns[:], in0=pos[:], scalar1=wfr[:, 2:3], scalar2=MAGIC, op0=ALU.mult, op1=ALU.add)
         nint = tmp.tile([P, S_LEN], I32, tag="t", name="nint")
         nc.vector.tensor_scalar(out=nint[:], in0=turns[:], scalar1=-MAGIC, scalar2=None, op0=ALU.add)
-        nc.vector.scalar_tensor_tensor(out=ang[:], in0=nint[:], scalar=-C1, in1=ang[:], op0=ALU.mult, op1=ALU.add)
-        nc.vector.scalar_tensor_tensor(out=ang[:], in0=nint[:], scalar=-C2, in1=ang[:], op0=ALU.mult, op1=ALU.add)
+        nc.vector.scalar_tensor_tensor(out=ang[:], in0=nint[:], scalar=-2.0 * PI, in1=ang[:], op0=ALU.mult, op1=ALU.add)
         mab = tmp.tile([P, S_LEN], F32, tag="t", name="mab")
         nc.vector.scalar_tensor_tensor(out=mab[:], in0=ang[:], scalar=-1.0, in1=ang[:], op0=ALU.mult, op1=ALU.min)
 
@@ -145,32 +143,32 @@ def tile_autoreggqaattention_pa_kernel(tc, hidden_states, Wq, bq, Wk, bk, Wv, bv
             return gpool.tile(shape, BF16, tag=tag, name=tag, bufs=bufs, align_bytes=64)
 
         def ilv_pass(eng, grp, g):
-            copy_on(eng, grp[:], raw[0][:, g, :, :].rearrange("p j w -> p w j"))
+            copy_on(eng, grp, raw[0][:, g, :, :].rearrange("p j w -> p w j"))
 
         def ilv_head(eng, grp, c, hh, w0, w1):
             src = raw[c][:, :, :, hh * DH + w0:hh * DH + w1]
             dst = grp[:, :, w0:w1, :]
-            if FAST:
+            if eng in FAST:
                 for g in range(G):
                     copy_on(eng, dst[:, g, :, :].rearrange("p (c i) j -> p c j i", i=4), src[:, g, :, :].rearrange("p j (c i) -> p c j i", i=4))
             else:
                 copy_on(eng, dst, src.rearrange("p g j w -> p g w j"))
 
-        def quant(grp_flat):
-            wc = cpool.tile([P, CH], U32, tag="wc", name="wc", align_bytes=64)
-            ws = cpool.tile([P, CH], U8, tag="ws", name="ws", align_bytes=64)
+        def quant(grp_flat, n):
+            wc = cpool.tile([P, n * CH], U32, tag="wc%d" % n, name="wc%d" % n, align_bytes=64)
+            ws = cpool.tile([P, n * CH], U8, tag="ws%d" % n, name="ws%d" % n, align_bytes=64)
             nc.vector.quantize_mx(out=wc[:].bitcast(E5), scales=ws[:], in_=grp_flat)
-            return wc, ws
+            return [(wc[:, i * CH:(i + 1) * CH], ws[:, i * CH:(i + 1) * CH]) for i in range(n)]
 
         codes = {}
         g0 = grp_tile("gs", 3, [P, CH, PACK])
-        ilv_pass("S", g0, 0)
+        ilv_pass("S", g0[:], 0)
         browf = const.tile([P, P], F32, name="browf")
         nc.vector.tensor_copy(out=browf[:], in_=brow[:])
         bps = psb.tile([P, P], F32, tag="tr", name="bps")
         nc.tensor.transpose(bps[:], browf[:], ident[:])
-        g1 = grp_tile("gm", 1, [P, CH, PACK])
-        ilv_pass("V", g1, 1)
+        g1 = grp_tile("gs", 3, [P, CH, PACK])
+        ilv_pass("V", g1[:], 1)
 
         sinh_ = tmp.tile([P, S_LEN], F32, tag="t", name="sinh_")
         nc.scalar.activation(out=sinh_[:], in_=ang[:], func=ACT.Sin, scale=0.5)
@@ -179,8 +177,8 @@ def tile_autoreggqaattention_pa_kernel(tc, hidden_states, Wq, bq, Wk, bk, Wv, bv
         cos_t = const.tile([P, S_LEN], F32, name="cos_t")
         nc.scalar.activation(out=cos_t[:], in_=mab[:], func=ACT.Sin, bias=halfpi[:, 0:1], scale=1.0)
 
-        codes[(0, 0)] = quant(g0[:].rearrange("p w j -> p (w j)"))
-        codes[(0, 1)] = quant(g1[:].rearrange("p w j -> p (w j)"))
+        codes[(0, 0)] = quant(g0[:].rearrange("p w j -> p (w j)"), 1)[0]
+        codes[(0, 1)] = quant(g1[:].rearrange("p w j -> p (w j)"), 1)[0]
         bias = const.tile([P, 32], F32, name="bias")
         nc.vector.tensor_copy(out=bias[:, 0:NH + 2 * NKV], in_=bps[:, 0:NH + 2 * NKV])
         sin_t = const.tile([P, S_LEN], F32, name="sin_t")
@@ -219,13 +217,11 @@ def tile_autoreggqaattention_pa_kernel(tc, hidden_states, Wq, bq, Wk, bk, Wv, bv
         x_quant(0)
         x_tile(2, "SV")
         x_tile(3, "SV")
-        g2t = grp_tile("gs", 3, [P, CH, PACK])
-        ilv_pass("S", g2t, 2)
+        g23 = grp_tile("gg", 1, [P, 2, CH, PACK])
+        ilv_pass("S", g23[:, 0, :, :], 2)
         x_quant(1)
-        g3t = grp_tile("gg", 1, [P, CH, PACK])
-        ilv_pass("V", g3t, 3)
-        codes[(0, 2)] = quant(g2t[:].rearrange("p w j -> p (w j)"))
-        codes[(0, 3)] = quant(g3t[:].rearrange("p w j -> p (w j)"))
+        ilv_pass("V", g23[:, 1, :, :], 3)
+        codes[(0, 2)], codes[(0, 3)] = quant(g23[:].rearrange("p n w j -> p (n w j)"), 2)
 
         acc = {}
         prod = {}
@@ -264,7 +260,7 @@ def tile_autoreggqaattention_pa_kernel(tc, hidden_states, Wq, bq, Wk, bk, Wv, bv
             a = acc[(c, hh)]
             ta = apool.tile([P, S_LEN], F32, tag="ta", name="ta")
             if c == NCHUNK - 1:
-                nc.vector.tensor_scalar(out=ta[:], in0=a[:], scalar1=bias_col(c, hh), scalar2=None, op0=ALU.add)
+                nc.scalar.activation(out=ta[:], in_=a[:], func=ACT.Identity, bias=bias_col(c, hh), scale=1.0)
                 prod[(c, hh)] = (ta,)
             else:
                 tb = apool.tile([P, S_LEN], F32, tag="tb", name="tb")
@@ -293,41 +289,34 @@ def tile_autoreggqaattention_pa_kernel(tc, hidden_states, Wq, bq, Wk, bk, Wv, bv
                 dst = out_0[0, (c - 1) * 4 + hh]
             o = opool.tile([P, S_LEN], F32, tag="o", name="o")
             nc.scalar.copy(out=o[:], in_=trb[(c, hh)][:])
-            nc.scalar.dma_start(out=dst.rearrange("(p t) d -> p (t d)", t=NT), in_=o[:])
+            nc.sync.dma_start(out=dst.rearrange("(p t) d -> p (t d)", t=NT), in_=o[:])
 
         for hh in range(4):
             mx(0, hh)
 
-        HS = [P, G, DH, PACK]
+        flat = "p g w j -> p (g w j)"
         for c in range(NCHUNK - 1):
             nx = c + 1
-            if c == 0:
-                alloc_raw(NCHUNK - 1)
+            if c + PRELOAD < NCHUNK:
+                alloc_raw(c + PRELOAD)
                 for g in range(G):
-                    load_w(NCHUNK - 1, g)
-            u0 = grp_tile("gs", 3, HS)
+                    load_w(c + PRELOAD, g)
+            u0 = grp_tile("gs", 3, [P, G, DH, PACK])
             ilv_head("S", u0, nx, 0, 0, DH)
-            u1 = grp_tile("gs", 3, HS)
+            u1 = grp_tile("gs", 3, [P, G, DH, PACK])
             ilv_head("S", u1, nx, 1, 0, DH)
-            u3 = grp_tile("gg", 1, HS)
-            u2 = grp_tile("gm", 1, HS)
-            if USE_G:
-                ilv_head("G", u3, nx, 3, 0, DH)
-                ilv_head("G", u2, nx, 2, 0, GCOLS)
+            u23 = grp_tile("gg", 1, [P, 2, G, DH, PACK])
+            ilv_head("G", u23[:, 1, :, :, :], nx, 3, 0, DH)
+            ilv_head("G", u23[:, 0, :, :, :], nx, 2, 0, GCOLS)
+            if SCOLS > 0:
+                ilv_head("S", u23[:, 0, :, :, :], nx, 2, GCOLS, GCOLS + SCOLS)
             for hh in range(4):
                 products(c, hh)
-            if USE_G:
-                ilv_head("V", u2, nx, 2, GCOLS, DH)
-            else:
-                ilv_head("V", u2, nx, 2, 0, DH)
-            flat = "p g w j -> p (g w j)"
-            codes[(nx, 0)] = quant(u0[:].rearrange(flat))
-            codes[(nx, 1)] = quant(u1[:].rearrange(flat))
-            if not USE_G:
-                ilv_head("V", u3, nx, 3, 0, 32)
-                ilv_head("S", u3, nx, 3, 32, DH)
-            codes[(nx, 2)] = quant(u2[:].rearrange(flat))
-            codes[(nx, 3)] = quant(u3[:].rearrange(flat))
+            if GCOLS + SCOLS < DH:
+                ilv_head("V", u23[:, 0, :, :, :], nx, 2, GCOLS + SCOLS, DH)
+            codes[(nx, 0)] = quant(u0[:].rearrange(flat), 1)[0]
+            codes[(nx, 1)] = quant(u1[:].rearrange(flat), 1)[0]
+            codes[(nx, 2)], codes[(nx, 3)] = quant(u23[:].rearrange("p n g w j -> p (n g w j)"), 2)
             for hh in range(4):
                 turn(c, hh)
             if nx < NCHUNK - 1:
@@ -339,9 +328,17 @@ def tile_autoreggqaattention_pa_kernel(tc, hidden_states, Wq, bq, Wk, bk, Wv, bv
         c = NCHUNK - 1
         mx(c, 0)
         mx(c, 1)
-        for hh in range(4):
-            products(c, hh)
-            turn(c, hh)
-            leave(c, hh)
-            if hh + 2 < 4:
-                mx(c, hh + 2)
+        products(c, 0)
+        turn(c, 0)
+        mx(c, 2)
+        products(c, 1)
+        leave(c, 0)
+        turn(c, 1)
+        mx(c, 3)
+        products(c, 2)
+        leave(c, 1)
+        turn(c, 2)
+        products(c, 3)
+        leave(c, 2)
+        turn(c, 3)
+        leave(c, 3)

@@ -28,7 +28,6 @@ MAGIC = 12582912.0
 THETA = 10000.0
 
 GCOLS = 96
-SCOLS = 32
 FAST = ''
 PRELOAD = 3
 
@@ -67,9 +66,6 @@ def tile_autoreggqaattention_pa_kernel(tc, hidden_states, Wq, bq, Wk, bk, Wv, bv
 
         brow = const.tile([P, P], BF16, name="brow")
         nc.gpsimd.memset(brow[:], 0.0)
-        nc.scalar.dma_start(out=brow[0:NH, :], in_=bq.rearrange("(h d) -> h d", d=DH))
-        nc.scalar.dma_start(out=brow[NH:NH + NKV, :], in_=bk.rearrange("(h d) -> h d", d=DH))
-        nc.scalar.dma_start(out=brow[NH + NKV:NH + 2 * NKV, :], in_=bv.rearrange("(h d) -> h d", d=DH))
 
         x_sb = const.tile([P, NT, H], BF16, name="x_sb")
         xv = hidden_states.rearrange("b (p t) k -> p (b t) k", t=NT)
@@ -80,6 +76,8 @@ def tile_autoreggqaattention_pa_kernel(tc, hidden_states, Wq, bq, Wk, bk, Wv, bv
             nc.sync.dma_start(out=x_sb[:, t, :], in_=xv[:, t, :])
         load_w(0, 2)
         load_w(0, 3)
+        nc.sync.dma_start(out=brow[0:NH, :], in_=bq.rearrange("(h d) -> h d", d=DH))
+        nc.sync.dma_start(out=brow[NH:NH + NKV, :], in_=bk.rearrange("(h d) -> h d", d=DH))
         for c in range(1, PRELOAD):
             alloc_raw(c)
             for g in range(G):
@@ -142,8 +140,8 @@ def tile_autoreggqaattention_pa_kernel(tc, hidden_states, Wq, bq, Wk, bk, Wv, bv
         def grp_tile(tag, bufs, shape):
             return gpool.tile(shape, BF16, tag=tag, name=tag, bufs=bufs, align_bytes=64)
 
-        def ilv_pass(eng, grp, g):
-            copy_on(eng, grp, raw[0][:, g, :, :].rearrange("p j w -> p w j"))
+        def ilv_pass(eng, grp, c, g, w0, w1):
+            copy_on(eng, grp[:, w0:w1, :], raw[c][:, g, :, w0:w1].rearrange("p j w -> p w j"))
 
         def ilv_head(eng, grp, c, hh, w0, w1):
             src = raw[c][:, :, :, hh * DH + w0:hh * DH + w1]
@@ -162,27 +160,11 @@ def tile_autoreggqaattention_pa_kernel(tc, hidden_states, Wq, bq, Wk, bk, Wv, bv
 
         codes = {}
         g0 = grp_tile("gs", 3, [P, CH, PACK])
-        ilv_pass("S", g0[:], 0)
-        browf = const.tile([P, P], F32, name="browf")
-        nc.vector.tensor_copy(out=browf[:], in_=brow[:])
-        bps = psb.tile([P, P], F32, tag="tr", name="bps")
-        nc.tensor.transpose(bps[:], browf[:], ident[:])
+        ilv_pass("S", g0, 0, 0, 0, CH)
         g1 = grp_tile("gs", 3, [P, CH, PACK])
-        ilv_pass("V", g1[:], 1)
-
-        sinh_ = tmp.tile([P, S_LEN], F32, tag="t", name="sinh_")
-        nc.scalar.activation(out=sinh_[:], in_=ang[:], func=ACT.Sin, scale=0.5)
-        cosh_ = tmp.tile([P, S_LEN], F32, tag="t", name="cosh_")
-        nc.scalar.activation(out=cosh_[:], in_=mab[:], func=ACT.Sin, bias=halfpi[:, 0:1], scale=0.5)
-        cos_t = const.tile([P, S_LEN], F32, name="cos_t")
-        nc.scalar.activation(out=cos_t[:], in_=mab[:], func=ACT.Sin, bias=halfpi[:, 0:1], scale=1.0)
-
+        ilv_pass("V", g1, 0, 1, 0, CH)
         codes[(0, 0)] = quant(g0[:].rearrange("p w j -> p (w j)"), 1)[0]
         codes[(0, 1)] = quant(g1[:].rearrange("p w j -> p (w j)"), 1)[0]
-        bias = const.tile([P, 32], F32, name="bias")
-        nc.vector.tensor_copy(out=bias[:, 0:NH + 2 * NKV], in_=bps[:, 0:NH + 2 * NKV])
-        sin_t = const.tile([P, S_LEN], F32, name="sin_t")
-        nc.vector.scalar_tensor_tensor(out=sin_t[:], in0=sinh_[:], scalar=sgn2[:, 0:1], in1=cosh_[:], op0=ALU.mult, op1=ALU.mult)
 
         xw = x_sb[:].bitcast(F32)
         xg = const.tile([P, G, S_LEN * PACK], BF16, name="xg", align_bytes=64)
@@ -213,15 +195,31 @@ def tile_autoreggqaattention_pa_kernel(tc, hidden_states, Wq, bq, Wk, bk, Wv, bv
                 )
 
         x_tile(0, "SS")
-        x_tile(1, "SV")
+        x_tile(1, "SS")
         x_quant(0)
-        x_tile(2, "SV")
-        x_tile(3, "SV")
+        x_tile(2, "SS")
+        x_tile(3, "SS")
         g23 = grp_tile("gg", 1, [P, 2, CH, PACK])
-        ilv_pass("S", g23[:, 0, :, :], 2)
+        ilv_pass("V", g23[:, 0, :, :], 0, 2, 0, CH)
         x_quant(1)
-        ilv_pass("V", g23[:, 1, :, :], 3)
+
+        sinh_ = tmp.tile([P, S_LEN], F32, tag="t", name="sinh_")
+        nc.scalar.activation(out=sinh_[:], in_=ang[:], func=ACT.Sin, scale=0.5)
+        cosh_ = tmp.tile([P, S_LEN], F32, tag="t", name="cosh_")
+        nc.scalar.activation(out=cosh_[:], in_=mab[:], func=ACT.Sin, bias=halfpi[:, 0:1], scale=0.5)
+        cos_t = const.tile([P, S_LEN], F32, name="cos_t")
+        nc.scalar.activation(out=cos_t[:], in_=mab[:], func=ACT.Sin, bias=halfpi[:, 0:1], scale=1.0)
+
+        browf = const.tile([P, P], F32, name="browf")
+        nc.vector.tensor_copy(out=browf[:], in_=brow[:])
+        bps = psb.tile([P, P], F32, tag="tr", name="bps")
+        nc.tensor.transpose(bps[:], browf[:], ident[:])
+        ilv_pass("V", g23[:, 1, :, :], 0, 3, 0, CH)
+        bias = const.tile([P, 32], F32, name="bias")
+        nc.vector.tensor_copy(out=bias[:, 0:NH + NKV], in_=bps[:, 0:NH + NKV])
         codes[(0, 2)], codes[(0, 3)] = quant(g23[:].rearrange("p n w j -> p (n w j)"), 2)
+        sin_t = const.tile([P, S_LEN], F32, name="sin_t")
+        nc.vector.scalar_tensor_tensor(out=sin_t[:], in0=sinh_[:], scalar=sgn2[:, 0:1], in1=cosh_[:], op0=ALU.mult, op1=ALU.mult)
 
         acc = {}
         prod = {}
@@ -248,25 +246,16 @@ def tile_autoreggqaattention_pa_kernel(tc, hidden_states, Wq, bq, Wk, bk, Wv, bv
                 )
 
         def bias_col(c, hh):
-            if c == 0:
-                k = NH + hh
-            elif c == NCHUNK - 1:
-                k = NH + NKV + hh
-            else:
-                k = (c - 1) * 4 + hh
+            k = NH + hh if c == 0 else (c - 1) * 4 + hh
             return bias[:, k:k + 1]
 
         def products(c, hh):
             a = acc[(c, hh)]
             ta = apool.tile([P, S_LEN], F32, tag="ta", name="ta")
-            if c == NCHUNK - 1:
-                nc.scalar.activation(out=ta[:], in_=a[:], func=ACT.Identity, bias=bias_col(c, hh), scale=1.0)
-                prod[(c, hh)] = (ta,)
-            else:
-                tb = apool.tile([P, S_LEN], F32, tag="tb", name="tb")
-                nc.vector.scalar_tensor_tensor(out=ta[:], in0=a[:], scalar=bias_col(c, hh), in1=cos_t[:], op0=ALU.add, op1=ALU.mult)
-                nc.vector.scalar_tensor_tensor(out=tb[:], in0=a[:], scalar=bias_col(c, hh), in1=sin_t[:], op0=ALU.add, op1=ALU.mult)
-                prod[(c, hh)] = (ta, tb)
+            tb = apool.tile([P, S_LEN], F32, tag="tb", name="tb")
+            nc.vector.scalar_tensor_tensor(out=ta[:], in0=a[:], scalar=bias_col(c, hh), in1=cos_t[:], op0=ALU.add, op1=ALU.mult)
+            nc.vector.scalar_tensor_tensor(out=tb[:], in0=a[:], scalar=bias_col(c, hh), in1=sin_t[:], op0=ALU.add, op1=ALU.mult)
+            prod[(c, hh)] = (ta, tb)
 
         def turn(c, hh):
             tr = psb.tile([P, S_LEN], F32, tag="tr", name="tr")
@@ -274,19 +263,11 @@ def tile_autoreggqaattention_pa_kernel(tc, hidden_states, Wq, bq, Wk, bk, Wv, bv
             pr = prod[(c, hh)]
             for t in range(NT):
                 blk = slice(t * P, (t + 1) * P)
-                if len(pr) == 1:
-                    nc.tensor.transpose(tr[:, blk], pr[0][:, blk], ident[:])
-                else:
-                    nc.tensor.matmul(out=tr[:, blk], lhsT=pr[0][:, blk], rhs=ident[:], is_transpose=True, start=True, stop=False)
-                    nc.tensor.matmul(out=tr[:, blk], lhsT=pr[1][:, blk], rhs=pswap[:], is_transpose=True, start=False, stop=True)
+                nc.tensor.matmul(out=tr[:, blk], lhsT=pr[0][:, blk], rhs=ident[:], is_transpose=True, start=True, stop=False)
+                nc.tensor.matmul(out=tr[:, blk], lhsT=pr[1][:, blk], rhs=pswap[:], is_transpose=True, start=False, stop=True)
 
         def leave(c, hh):
-            if c == 0:
-                dst = out_1[0, hh]
-            elif c == NCHUNK - 1:
-                dst = out_2[0, hh]
-            else:
-                dst = out_0[0, (c - 1) * 4 + hh]
+            dst = out_1[0, hh] if c == 0 else out_0[0, (c - 1) * 4 + hh]
             o = opool.tile([P, S_LEN], F32, tag="o", name="o")
             nc.scalar.copy(out=o[:], in_=trb[(c, hh)][:])
             nc.sync.dma_start(out=dst.rearrange("(p t) d -> p (t d)", t=NT), in_=o[:])
@@ -294,51 +275,71 @@ def tile_autoreggqaattention_pa_kernel(tc, hidden_states, Wq, bq, Wk, bk, Wv, bv
         for hh in range(4):
             mx(0, hh)
 
-        flat = "p g w j -> p (g w j)"
+        bvb = const.tile([P, NKV * DH], BF16, name="bvb")
+        accv = []
         for c in range(NCHUNK - 1):
             nx = c + 1
+            v_next = nx == NCHUNK - 1
             if c + PRELOAD < NCHUNK:
                 alloc_raw(c + PRELOAD)
                 for g in range(G):
                     load_w(c + PRELOAD, g)
-            u0 = grp_tile("gs", 3, [P, G, DH, PACK])
-            ilv_head("S", u0, nx, 0, 0, DH)
-            u1 = grp_tile("gs", 3, [P, G, DH, PACK])
-            ilv_head("S", u1, nx, 1, 0, DH)
-            u23 = grp_tile("gg", 1, [P, 2, G, DH, PACK])
-            ilv_head("G", u23[:, 1, :, :, :], nx, 3, 0, DH)
-            ilv_head("G", u23[:, 0, :, :, :], nx, 2, 0, GCOLS)
-            if SCOLS > 0:
-                ilv_head("S", u23[:, 0, :, :, :], nx, 2, GCOLS, GCOLS + SCOLS)
+            if c == 1:
+                nc.sync.dma_start(out=bvb[:], in_=bv.partition_broadcast(P))
+            if v_next:
+                u0 = grp_tile("gs", 3, [P, CH, PACK])
+                ilv_pass("S", u0, nx, 0, 0, CH)
+                u1 = grp_tile("gs", 3, [P, CH, PACK])
+                ilv_pass("S", u1, nx, 1, 0, CH)
+                u23 = grp_tile("gg", 1, [P, 2, CH, PACK])
+                ilv_pass("G", u23[:, 1, :, :], nx, 3, 0, CH)
+                ilv_pass("G", u23[:, 0, :, :], nx, 2, 0, 4 * GCOLS)
+                ilv_pass("S", u23[:, 0, :, :], nx, 2, 4 * GCOLS, CH)
+                flat1 = "p w j -> p (w j)"
+                flat2 = "p n w j -> p (n w j)"
+            else:
+                u0 = grp_tile("gs", 3, [P, G, DH, PACK])
+                ilv_head("S", u0, nx, 0, 0, DH)
+                u1 = grp_tile("gs", 3, [P, G, DH, PACK])
+                ilv_head("S", u1, nx, 1, 0, DH)
+                u23 = grp_tile("gg", 1, [P, 2, G, DH, PACK])
+                ilv_head("G", u23[:, 1, :, :, :], nx, 3, 0, DH)
+                ilv_head("G", u23[:, 0, :, :, :], nx, 2, 0, GCOLS)
+                ilv_head("S", u23[:, 0, :, :, :], nx, 2, GCOLS, DH)
+                flat1 = "p g w j -> p (g w j)"
+                flat2 = "p n g w j -> p (n g w j)"
             for hh in range(4):
                 products(c, hh)
-            if GCOLS + SCOLS < DH:
-                ilv_head("V", u23[:, 0, :, :, :], nx, 2, GCOLS + SCOLS, DH)
-            codes[(nx, 0)] = quant(u0[:].rearrange(flat), 1)[0]
-            codes[(nx, 1)] = quant(u1[:].rearrange(flat), 1)[0]
-            codes[(nx, 2)], codes[(nx, 3)] = quant(u23[:].rearrange("p n g w j -> p (n g w j)"), 2)
+            codes[(nx, 0)] = quant(u0[:].rearrange(flat1), 1)[0]
+            codes[(nx, 1)] = quant(u1[:].rearrange(flat1), 1)[0]
+            codes[(nx, 2)], codes[(nx, 3)] = quant(u23[:].rearrange(flat2), 2)
             for hh in range(4):
                 turn(c, hh)
-            if nx < NCHUNK - 1:
+            if v_next:
+                for t in range(NT):
+                    av = psa.tile([P, NKV * DH], F32, tag="acc", name="accv")
+                    accv.append(av)
+                order = [(g, t) for g in (0, 1) for t in range(NT)] + [(g, t) for t in range(NT) for g in (2, 3)]
+                for g, t in order:
+                    wc, ws = codes[(nx, g)]
+                    blk = slice(t * P, (t + 1) * P)
+                    nc.tensor.matmul_mx(
+                        out=accv[t][:],
+                        lhsT=xc[:, g, blk].bitcast(E5),
+                        lhsT_scale=xs[:, g, blk],
+                        rhs=wc.bitcast(E5),
+                        rhs_scale=ws,
+                        start=(g == 0),
+                        stop=(g == G - 1),
+                    )
+            else:
                 for hh in range(4):
                     mx(nx, hh)
             for hh in range(4):
                 leave(c, hh)
 
-        c = NCHUNK - 1
-        mx(c, 0)
-        mx(c, 1)
-        products(c, 0)
-        turn(c, 0)
-        mx(c, 2)
-        products(c, 1)
-        leave(c, 0)
-        turn(c, 1)
-        mx(c, 3)
-        products(c, 2)
-        leave(c, 1)
-        turn(c, 2)
-        products(c, 3)
-        leave(c, 2)
-        turn(c, 3)
-        leave(c, 3)
+        vdst = out_2[0].rearrange("h (p t) d -> t p h d", t=NT)
+        for t in range(NT):
+            o = opool.tile([P, NKV * DH], F32, tag="o", name="o")
+            nc.vector.tensor_tensor(out=o[:], in0=accv[t][:], in1=bvb[:], op=ALU.add)
+            nc.sync.dma_start(out=vdst[t], in_=o[:].rearrange("p (h d) -> p h d", h=NKV))

@@ -41,7 +41,7 @@ def tile_autoreggqaattention_pa_kernel(tc, hidden_states, Wq, bq, Wk, bk, Wv, bv
         gpool = ctx.enter_context(tc.tile_pool(name="gpool", bufs=1))
         cpool = ctx.enter_context(tc.tile_pool(name="cpool", bufs=4))
         apool = ctx.enter_context(tc.tile_pool(name="apool", bufs=4))
-        opool = ctx.enter_context(tc.tile_pool(name="opool", bufs=4))
+        opool = ctx.enter_context(tc.tile_pool(name="opool", bufs=8))
         psa = ctx.enter_context(tc.psum_pool(name="psa", bufs=4))
         psb = ctx.enter_context(tc.psum_pool(name="psb", bufs=4))
         ctx.enter_context(tc.manual_schedule())
@@ -78,6 +78,7 @@ def tile_autoreggqaattention_pa_kernel(tc, hidden_states, Wq, bq, Wk, bk, Wv, bv
         load_w(0, 3)
         nc.sync.dma_start(out=brow[0:NH, :], in_=bq.rearrange("(h d) -> h d", d=DH))
         nc.sync.dma_start(out=brow[NH:NH + NKV, :], in_=bk.rearrange("(h d) -> h d", d=DH))
+        nc.sync.dma_start(out=brow[NH + NKV:NH + 2 * NKV, :], in_=bv.rearrange("(h d) -> h d", d=DH))
         for c in range(1, PRELOAD):
             alloc_raw(c)
             for g in range(G):
@@ -201,7 +202,13 @@ def tile_autoreggqaattention_pa_kernel(tc, hidden_states, Wq, bq, Wk, bk, Wv, bv
         x_tile(3, "SS")
         g23 = grp_tile("gg", 1, [P, 2, CH, PACK])
         ilv_pass("V", g23[:, 0, :, :], 0, 2, 0, CH)
+        browf = const.tile([P, P], F32, name="browf")
+        nc.vector.tensor_copy(out=browf[:], in_=brow[:])
+        bps = psb.tile([P, P], F32, tag="tr", name="bps")
+        nc.tensor.transpose(bps[:], browf[:], ident[:])
         x_quant(1)
+        bias = const.tile([P, 32], F32, name="bias")
+        nc.vector.tensor_copy(out=bias[:, 0:NH + 2 * NKV], in_=bps[:, 0:NH + 2 * NKV])
 
         sinh_ = tmp.tile([P, S_LEN], F32, tag="t", name="sinh_")
         nc.scalar.activation(out=sinh_[:], in_=ang[:], func=ACT.Sin, scale=0.5)
@@ -210,13 +217,13 @@ def tile_autoreggqaattention_pa_kernel(tc, hidden_states, Wq, bq, Wk, bk, Wv, bv
         cos_t = const.tile([P, S_LEN], F32, name="cos_t")
         nc.scalar.activation(out=cos_t[:], in_=mab[:], func=ACT.Sin, bias=halfpi[:, 0:1], scale=1.0)
 
-        browf = const.tile([P, P], F32, name="browf")
-        nc.vector.tensor_copy(out=browf[:], in_=brow[:])
-        bps = psb.tile([P, P], F32, tag="tr", name="bps")
-        nc.tensor.transpose(bps[:], browf[:], ident[:])
+        bvp = psb.tile([P, NKV * DH], F32, tag="tr", name="bvp")
+        for hh in range(NKV):
+            k = NH + NKV + hh
+            nc.tensor.matmul(out=bvp[:, hh * DH:(hh + 1) * DH], lhsT=bias[:, k:k + 1].to_broadcast([P, P]), rhs=ident[:], start=True, stop=True)
+        bvb = const.tile([P, NKV * DH], F32, name="bvb")
+        nc.scalar.copy(out=bvb[:], in_=bvp[:])
         ilv_pass("V", g23[:, 1, :, :], 0, 3, 0, CH)
-        bias = const.tile([P, 32], F32, name="bias")
-        nc.vector.tensor_copy(out=bias[:, 0:NH + NKV], in_=bps[:, 0:NH + NKV])
         codes[(0, 2)], codes[(0, 3)] = quant(g23[:].rearrange("p n w j -> p (n w j)"), 2)
         sin_t = const.tile([P, S_LEN], F32, name="sin_t")
         nc.vector.scalar_tensor_tensor(out=sin_t[:], in0=sinh_[:], scalar=sgn2[:, 0:1], in1=cosh_[:], op0=ALU.mult, op1=ALU.mult)
@@ -275,7 +282,6 @@ def tile_autoreggqaattention_pa_kernel(tc, hidden_states, Wq, bq, Wk, bk, Wv, bv
         for hh in range(4):
             mx(0, hh)
 
-        bvb = const.tile([P, NKV * DH], BF16, name="bvb")
         accv = []
         for c in range(NCHUNK - 1):
             nx = c + 1
@@ -284,8 +290,6 @@ def tile_autoreggqaattention_pa_kernel(tc, hidden_states, Wq, bq, Wk, bk, Wv, bv
                 alloc_raw(c + PRELOAD)
                 for g in range(G):
                     load_w(c + PRELOAD, g)
-            if c == 1:
-                nc.sync.dma_start(out=bvb[:], in_=bv.partition_broadcast(P))
             if v_next:
                 u0 = grp_tile("gs", 3, [P, CH, PACK])
                 ilv_pass("S", u0, nx, 0, 0, CH)

@@ -154,8 +154,8 @@ def tile_autoreggqaattention_pa_kernel(tc, hidden_states, Wq, bq, Wk, bk, Wv, bv
                 copy_on(eng, dst, src.rearrange("p g j w -> p g w j"))
 
         def quant(grp_flat, n):
-            wc = cpool.tile([P, n * CH], U32, tag="wc%d" % n, name="wc%d" % n, align_bytes=64)
-            ws = cpool.tile([P, n * CH], U8, tag="ws%d" % n, name="ws%d" % n, align_bytes=64)
+            wc = cpool.tile([P, n * CH], U32, tag="wc%d" % n, name="wc%d" % n, align_bytes=256)
+            ws = cpool.tile([P, n * CH], U8, tag="ws%d" % n, name="ws%d" % n, align_bytes=256)
             nc.vector.quantize_mx(out=wc[:].bitcast(E5), scales=ws[:], in_=grp_flat)
             return [(wc[:, i * CH:(i + 1) * CH], ws[:, i * CH:(i + 1) * CH]) for i in range(n)]
 
@@ -170,8 +170,8 @@ def tile_autoreggqaattention_pa_kernel(tc, hidden_states, Wq, bq, Wk, bk, Wv, bv
         xw = x_sb[:].bitcast(F32)
         xg = const.tile([P, G, S_LEN * PACK], BF16, name="xg", align_bytes=64)
         xgw = xg[:].bitcast(F32).rearrange("p g (r u) -> p g r u", u=2)
-        xc = const.tile([P, G, S_LEN], U32, name="xc", align_bytes=64)
-        xs = const.tile([P, G, S_LEN], U8, name="xs", align_bytes=64)
+        xc = const.tile([P, G, S_LEN], U32, name="xc", align_bytes=256)
+        xs = const.tile([P, G, S_LEN], U8, name="xs", align_bytes=256)
 
         def x_tile(t, engs):
             for gp in range(2):

@@ -298,7 +298,6 @@ def tile_autoreggqaattention_pa_kernel(tc, hidden_states, Wq, bq, Wk, bk, Wv, bv
                 u23 = grp_tile("gg", 1, [P, 2, CH, PACK])
                 ilv_pass("G", u23[:, 1, :, :], nx, 3, 0, CH)
                 ilv_pass("G", u23[:, 0, :, :], nx, 2, 0, 4 * GCOLS)
-                ilv_pass("S", u23[:, 0, :, :], nx, 2, 4 * GCOLS, CH)
                 flat1 = "p w j -> p (w j)"
                 flat2 = "p n w j -> p (n w j)"
             else:
@@ -309,12 +308,15 @@ def tile_autoreggqaattention_pa_kernel(tc, hidden_states, Wq, bq, Wk, bk, Wv, bv
                 u23 = grp_tile("gg", 1, [P, 2, G, DH, PACK])
                 ilv_head("G", u23[:, 1, :, :, :], nx, 3, 0, DH)
                 ilv_head("G", u23[:, 0, :, :, :], nx, 2, 0, GCOLS)
-                ilv_head("S", u23[:, 0, :, :, :], nx, 2, GCOLS, DH)
                 flat1 = "p g w j -> p (g w j)"
                 flat2 = "p n g w j -> p (n g w j)"
             for hh in range(4):
                 products(c, hh)
             codes[(nx, 0)] = quant(u0[:].rearrange(flat1), 1)[0]
+            if v_next:
+                ilv_pass("V", u23[:, 0, :, :], nx, 2, 4 * GCOLS, CH)
+            else:
+                ilv_head("V", u23[:, 0, :, :, :], nx, 2, GCOLS, DH)
             codes[(nx, 1)] = quant(u1[:].rearrange(flat1), 1)[0]
             codes[(nx, 2)], codes[(nx, 3)] = quant(u23[:].rearrange(flat2), 2)
             for hh in range(4):

@@ -27,7 +27,7 @@ PI = 3.141592653589793
 MAGIC = 12582912.0
 THETA = 10000.0
 
-GCOLS = 96
+GCOLS = 72
 FAST = ''
 PRELOAD = 3
 

@@ -348,4 +348,5 @@ def tile_autoreggqaattention_pa_kernel(tc, hidden_states, Wq, bq, Wk, bk, Wv, bv
         for t in range(NT):
             o = opool.tile([P, NKV * DH], F32, tag="o", name="o")
             nc.vector.tensor_tensor(out=o[:], in0=accv[t][:], in1=bvb[:], op=ALU.add)
-            nc.sync.dma_start(out=vdst[t], in_=o[:].rearrange("p (h d) -> p h d", h=NKV))
+            queue = nc.sync if t % 2 == 0 else nc.scalar
+            queue.dma_start(out=vdst[t], in_=o[:].rearrange("p (h d) -> p h d", h=NKV))

from contextlib import ExitStack

import concourse.mybir as mybir
from concourse.masks import make_identity

S_LEN, H, NH, NKV, DH = 512, 2048, 16, 4, 128
FLOPS = 2 * S_LEN * H * (NH + 2 * NKV) * DH

F32 = mybir.dt.float32
BF16 = mybir.dt.bfloat16
U32 = mybir.dt.uint32
U8 = mybir.dt.uint8
I32 = mybir.dt.int32
E5 = mybir.dt.float8_e5m2_x4
ALU = mybir.AluOpType
ACT = mybir.ActivationFunctionType

P = 128
PACK = 4
K_PASS = P * PACK
G = H // K_PASS
NT = S_LEN // P
CH = 512
NCHUNK = 6

PI = 3.141592653589793
MAGIC = 12582912.0
THETA = 10000.0

GCOLS = 72
FAST = ''
PRELOAD = 3


def tile_autoreggqaattention_pa_kernel(tc, hidden_states, Wq, bq, Wk, bk, Wv, bv, out_0, out_1, out_2):
    nc = tc.nc
    with ExitStack() as ctx:
        const = ctx.enter_context(tc.tile_pool(name="const", bufs=1))
        tmp = ctx.enter_context(tc.tile_pool(name="tmp", bufs=4))
        rawp = ctx.enter_context(tc.tile_pool(name="rawp", bufs=4))
        gpool = ctx.enter_context(tc.tile_pool(name="gpool", bufs=1))
        cpool = ctx.enter_context(tc.tile_pool(name="cpool", bufs=4))
        apool = ctx.enter_context(tc.tile_pool(name="apool", bufs=4))
        opool = ctx.enter_context(tc.tile_pool(name="opool", bufs=8))
        psa = ctx.enter_context(tc.psum_pool(name="psa", bufs=4))
        psb = ctx.enter_context(tc.psum_pool(name="psb", bufs=4))
        ctx.enter_context(tc.manual_schedule())

        def w_rows(c, g):
            rows = slice(g * K_PASS, (g + 1) * K_PASS)
            if c == 0:
                src = Wk[rows, :]
            elif c == NCHUNK - 1:
                src = Wv[rows, :]
            else:
                src = Wq[rows, (c - 1) * CH:c * CH]
            return src.rearrange("(p j) w -> p j w", j=PACK)

        raw = {}

        def alloc_raw(c):
            raw[c] = rawp.tile([P, G, PACK, CH], BF16, tag="raw", name="raw%d" % c)

        def load_w(c, g):
            nc.sync.dma_start(out=raw[c][:, g, :, :], in_=w_rows(c, g))

        brow = const.tile([P, P], BF16, name="brow")
        nc.gpsimd.memset(brow[:], 0.0)

        x_sb = const.tile([P, NT, H], BF16, name="x_sb")
        xv = hidden_states.rearrange("b (p t) k -> p (b t) k", t=NT)
        alloc_raw(0)
        load_w(0, 0)
        load_w(0, 1)
        for t in range(NT):
            nc.sync.dma_start(out=x_sb[:, t, :], in_=xv[:, t, :])
        load_w(0, 2)
        load_w(0, 3)
        nc.sync.dma_start(out=brow[0:NH, :], in_=bq.rearrange("(h d) -> h d", d=DH))
        nc.sync.dma_start(out=brow[NH:NH + NKV, :], in_=bk.rearrange("(h d) -> h d", d=DH))
        nc.sync.dma_start(out=brow[NH + NKV:NH + 2 * NKV, :], in_=bv.rearrange("(h d) -> h d", d=DH))
        for c in range(1, PRELOAD):
            alloc_raw(c)
            for g in range(G):
                load_w(c, g)

        zero1 = const.tile([P, 1], F32, name="zero1")
        nc.gpsimd.memset(zero1[:], 0.0)
        warm = const.tile([P, 1], F32, name="warm")
        nc.scalar.activation(out=warm[:], in_=zero1[:], func=ACT.Sin)

        idxn = const.tile([P, 8], I32, name="idxn")
        nc.gpsimd.iota(idxn[:], pattern=[[0, 8]], base=P - 1, channel_multiplier=-1)
        colj = const.tile([P, 8], I32, name="colj")
        nc.gpsimd.iota(colj[:], pattern=[[1, 8]], base=0, channel_multiplier=0)
        pos = tmp.tile([P, S_LEN], F32, tag="t", name="pos")
        nc.gpsimd.iota(pos[:], pattern=[[1, NT], [NT, P]], base=0, channel_multiplier=0, allow_small_or_imprecise_dtypes=True)
        ident = const.tile([P, P], F32, name="ident")
        make_identity(nc, ident[:])
        pswap = const.tile([P, P], F32, name="pswap")
        nc.gpsimd.tensor_copy(out=pswap[:, 0:64], in_=ident[:, 64:128])
        nc.gpsimd.tensor_copy(out=pswap[:, 64:128], in_=ident[:, 0:64])

        shf = const.tile([P, 8], I32, name="shf")
        nc.vector.tensor_tensor(out=shf[:], in0=idxn[:], in1=colj[:], op=ALU.logical_shift_right)
        nbit = const.tile([P, 8], I32, name="nbit")
        nc.vector.tensor_single_scalar(out=nbit[:], in_=shf[:], scalar=1, op=ALU.bitwise_and)
        fac = const.tile([P, 8], F32, name="fac")
        for j in range(6):
            gj = THETA ** (-(2.0 ** j) / 64.0)
            nc.vector.tensor_scalar(out=fac[:, j:j + 1], in0=nbit[:, j:j + 1], scalar1=1.0 - gj, scalar2=gj, op0=ALU.mult, op1=ALU.add)
        sgn2 = const.tile([P, 1], F32, name="sgn2")
        nc.vector.tensor_scalar(out=sgn2[:], in0=nbit[:, 6:7], scalar1=4.0, scalar2=-2.0, op0=ALU.mult, op1=ALU.add)
        halfpi = const.tile([P, 1], F32, name="halfpi")
        nc.vector.tensor_scalar(out=halfpi[:], in0=nbit[:, 6:7], scalar1=0.0, scalar2=PI / 2.0, op0=ALU.mult, op1=ALU.add)
        pr3 = const.tile([P, 4], F32, name="pr3")
        nc.vector.tensor_tensor(out=pr3[:, 0:3], in0=fac[:, 0:3], in1=fac[:, 3:6], op=ALU.mult)
        wfr = const.tile([P, 4], F32, name="wfr")
        nc.vector.tensor_tensor(out=wfr[:, 0:1], in0=pr3[:, 0:1], in1=pr3[:, 1:2], op=ALU.mult)
        nc.vector.tensor_tensor(out=wfr[:, 1:2], in0=wfr[:, 0:1], in1=pr3[:, 2:3], op=ALU.mult)
        nc.vector.tensor_scalar(out=wfr[:, 2:3], in0=wfr[:, 1:2], scalar1=1.0 / (2.0 * PI), scalar2=None, op0=ALU.mult)

        ang = tmp.tile([P, S_LEN], F32, tag="t", name="ang")
        nc.scalar.activation(out=ang[:], in_=pos[:], func=ACT.Identity, scale=wfr[:, 1:2])
        turns = tmp.tile([P, S_LEN], F32, tag="t", name="turns")
        nc.vector.tensor_scalar(out=turns[:], in0=pos[:], scalar1=wfr[:, 2:3], scalar2=MAGIC, op0=ALU.mult, op1=ALU.add)
        nint = tmp.tile([P, S_LEN], I32, tag="t", name="nint")
        nc.vector.tensor_scalar(out=nint[:], in0=turns[:], scalar1=-MAGIC, scalar2=None, op0=ALU.add)
        nc.vector.scalar_tensor_tensor(out=ang[:], in0=nint[:], scalar=-2.0 * PI, in1=ang[:], op0=ALU.mult, op1=ALU.add)
        mab = tmp.tile([P, S_LEN], F32, tag="t", name="mab")
        nc.vector.scalar_tensor_tensor(out=mab[:], in0=ang[:], scalar=-1.0, in1=ang[:], op0=ALU.mult, op1=ALU.min)

        def copy_on(eng, out, in_):
            if eng == "V":
                nc.vector.tensor_copy(out=out, in_=in_)
            elif eng == "S":
                nc.scalar.copy(out=out, in_=in_)
            else:
                nc.gpsimd.tensor_scalar(out=out, in0=in_, scalar1=1.0, scalar2=0.0, op0=ALU.mult, op1=ALU.add)

        def grp_tile(tag, bufs, shape):
            return gpool.tile(shape, BF16, tag=tag, name=tag, bufs=bufs, align_bytes=64)

        def ilv_pass(eng, grp, c, g, w0, w1):
            copy_on(eng, grp[:, w0:w1, :], raw[c][:, g, :, w0:w1].rearrange("p j w -> p w j"))

        def ilv_head(eng, grp, c, hh, w0, w1):
            src = raw[c][:, :, :, hh * DH + w0:hh * DH + w1]
            dst = grp[:, :, w0:w1, :]
            if eng in FAST:
                for g in range(G):
                    copy_on(eng, dst[:, g, :, :].rearrange("p (c i) j -> p c j i", i=4), src[:, g, :, :].rearrange("p j (c i) -> p c j i", i=4))
            else:
                copy_on(eng, dst, src.rearrange("p g j w -> p g w j"))

        def quant(grp_flat, n):
            wc = cpool.tile([P, n * CH], U32, tag="wc%d" % n, name="wc%d" % n, align_bytes=256)
            ws = cpool.tile([P, n * CH], U8, tag="ws%d" % n, name="ws%d" % n, align_bytes=256)
            nc.vector.quantize_mx(out=wc[:].bitcast(E5), scales=ws[:], in_=grp_flat)
            return [(wc[:, i * CH:(i + 1) * CH], ws[:, i * CH:(i + 1) * CH]) for i in range(n)]

        codes = {}
        g0 = grp_tile("gs", 3, [P, CH, PACK])
        ilv_pass("S", g0, 0, 0, 0, CH)
        g1 = grp_tile("gs", 3, [P, CH, PACK])
        ilv_pass("V", g1, 0, 1, 0, CH)
        codes[(0, 0)] = quant(g0[:].rearrange("p w j -> p (w j)"), 1)[0]
        codes[(0, 1)] = quant(g1[:].rearrange("p w j -> p (w j)"), 1)[0]

        xw = x_sb[:].bitcast(F32)
        xg = const.tile([P, G, S_LEN * PACK], BF16, name="xg", align_bytes=64)
        xgw = xg[:].bitcast(F32).rearrange("p g (r u) -> p g r u", u=2)
        xc = const.tile([P, G, S_LEN], U32, name="xc", align_bytes=256)
        xs = const.tile([P, G, S_LEN], U8, name="xs", align_bytes=256)

        def x_tile(t, engs):
            for gp in range(2):
                bank = psb.tile([P, 2, 2, P], F32, tag="tr", name="xbank")
                for g2 in range(2):
                    w0 = 256 * (2 * gp + g2)
                    for u in range(2):
                        nc.tensor.transpose(bank[:, g2, u, :], xw[:, t, w0 + u:w0 + 256:2], ident[:])
                dst = xgw[:, 2 * gp:2 * gp + 2, t * P:(t + 1) * P, :]
                src = bank[:].rearrange("p g u r -> p g r u")
                if engs[gp] == "S":
                    nc.scalar.copy(out=dst, in_=src)
                else:
                    nc.vector.tensor_copy(out=dst, in_=src)

        def x_quant(tp):
            for g in range(G):
                nc.vector.quantize_mx(
                    out=xc[:, g, tp * 256:(tp + 1) * 256].bitcast(E5),
                    scales=xs[:, g, tp * 256:(tp + 1) * 256],
                    in_=xg[:, g, tp * 1024:(tp + 1) * 1024],
                )

        x_tile(0, "SS")
        x_tile(1, "SS")
        x_quant(0)
        x_tile(2, "SS")
        x_tile(3, "SS")
        g23 = grp_tile("gg", 1, [P, 2, CH, PACK])
        ilv_pass("V", g23[:, 0, :, :], 0, 2, 0, CH)
        browf = const.tile([P, P], F32, name="browf")
        nc.vector.tensor_copy(out=browf[:], in_=brow[:])
        bps = psb.tile([P, P], F32, tag="tr", name="bps")
        nc.tensor.transpose(bps[:], browf[:], ident[:])
        x_quant(1)
        bias = const.tile([P, 32], F32, name="bias")
        nc.vector.tensor_copy(out=bias[:, 0:NH + 2 * NKV], in_=bps[:, 0:NH + 2 * NKV])

        sinh_ = tmp.tile([P, S_LEN], F32, tag="t", name="sinh_")
        nc.scalar.activation(out=sinh_[:], in_=ang[:], func=ACT.Sin, scale=0.5)
        cosh_ = tmp.tile([P, S_LEN], F32, tag="t", name="cosh_")
        nc.scalar.activation(out=cosh_[:], in_=mab[:], func=ACT.Sin, bias=halfpi[:, 0:1], scale=0.5)
        cos_t = const.tile([P, S_LEN], F32, name="cos_t")
        nc.scalar.activation(out=cos_t[:], in_=mab[:], func=ACT.Sin, bias=halfpi[:, 0:1], scale=1.0)

        bvp = psb.tile([P, NKV * DH], F32, tag="tr", name="bvp")
        for hh in range(NKV):
            k = NH + NKV + hh
            nc.tensor.matmul(out=bvp[:, hh * DH:(hh + 1) * DH], lhsT=bias[:, k:k + 1].to_broadcast([P, P]), rhs=ident[:], start=True, stop=True)
        bvb = const.tile([P, NKV * DH], F32, name="bvb")
        nc.scalar.copy(out=bvb[:], in_=bvp[:])
        ilv_pass("V", g23[:, 1, :, :], 0, 3, 0, CH)
        codes[(0, 2)], codes[(0, 3)] = quant(g23[:].rearrange("p n w j -> p (n w j)"), 2)
        sin_t = const.tile([P, S_LEN], F32, name="sin_t")
        nc.vector.scalar_tensor_tensor(out=sin_t[:], in0=sinh_[:], scalar=sgn2[:, 0:1], in1=cosh_[:], op0=ALU.mult, op1=ALU.mult)

        acc = {}
        prod = {}
        trb = {}

        def mx(c, hh):
            a = psa.tile([P, S_LEN], F32, tag="acc", name="acc")
            acc[(c, hh)] = a
            for g in range(G):
                if c == 0:
                    wc, ws = codes[(0, g)]
                    cols = slice(hh * DH, (hh + 1) * DH)
                else:
                    wc, ws = codes[(c, hh)]
                    cols = slice(g * DH, (g + 1) * DH)
                nc.tensor.matmul_mx(
                    out=a[:],
                    lhsT=wc[:, cols].bitcast(E5),
                    lhsT_scale=ws[:, cols],
                    rhs=xc[:, g, :].bitcast(E5),
                    rhs_scale=xs[:, g, :],
                    start=(g == 0),
                    stop=(g == G - 1),
                )

        def bias_col(c, hh):
            k = NH + hh if c == 0 else (c - 1) * 4 + hh
            return bias[:, k:k + 1]

        def products(c, hh):
            a = acc[(c, hh)]
            ta = apool.tile([P, S_LEN], F32, tag="ta", name="ta")
            tb = apool.tile([P, S_LEN], F32, tag="tb", name="tb")
            nc.vector.scalar_tensor_tensor(out=ta[:], in0=a[:], scalar=bias_col(c, hh), in1=cos_t[:], op0=ALU.add, op1=ALU.mult)
            nc.vector.scalar_tensor_tensor(out=tb[:], in0=a[:], scalar=bias_col(c, hh), in1=sin_t[:], op0=ALU.add, op1=ALU.mult)
            prod[(c, hh)] = (ta, tb)

        def turn(c, hh):
            tr = psb.tile([P, S_LEN], F32, tag="tr", name="tr")
            trb[(c, hh)] = tr
            pr = prod[(c, hh)]
            for t in range(NT):
                blk = slice(t * P, (t + 1) * P)
                nc.tensor.matmul(out=tr[:, blk], lhsT=pr[0][:, blk], rhs=ident[:], is_transpose=True, start=True, stop=False)
                nc.tensor.matmul(out=tr[:, blk], lhsT=pr[1][:, blk], rhs=pswap[:], is_transpose=True, start=False, stop=True)

        def leave(c, hh):
            dst = out_1[0, hh] if c == 0 else out_0[0, (c - 1) * 4 + hh]
            o = opool.tile([P, S_LEN], F32, tag="o", name="o")
            nc.scalar.copy(out=o[:], in_=trb[(c, hh)][:])
            nc.sync.dma_start(out=dst.rearrange("(p t) d -> p (t d)", t=NT), in_=o[:])

        for hh in range(4):
            mx(0, hh)

        accv = []
        for c in range(NCHUNK - 1):
            nx = c + 1
            v_next = nx == NCHUNK - 1
            if c + PRELOAD < NCHUNK:
                alloc_raw(c + PRELOAD)
                for g in range(G):
                    load_w(c + PRELOAD, g)
            if v_next:
                u0 = grp_tile("gs", 3, [P, CH, PACK])
                ilv_pass("S", u0, nx, 0, 0, CH)
                u1 = grp_tile("gs", 3, [P, CH, PACK])
                ilv_pass("S", u1, nx, 1, 0, CH)
                u23 = grp_tile("gg", 1, [P, 2, CH, PACK])
                ilv_pass("G", u23[:, 1, :, :], nx, 3, 0, CH)
                ilv_pass("G", u23[:, 0, :, :], nx, 2, 0, 4 * GCOLS)
                flat1 = "p w j -> p (w j)"
                flat2 = "p n w j -> p (n w j)"
            else:
                u0 = grp_tile("gs", 3, [P, G, DH, PACK])
                ilv_head("S", u0, nx, 0, 0, DH)
                u1 = grp_tile("gs", 3, [P, G, DH, PACK])
                ilv_head("S", u1, nx, 1, 0, DH)
                u23 = grp_tile("gg", 1, [P, 2, G, DH, PACK])
                ilv_head("G", u23[:, 1, :, :, :], nx, 3, 0, DH)
                ilv_head("G", u23[:, 0, :, :, :], nx, 2, 0, GCOLS)
                flat1 = "p g w j -> p (g w j)"
                flat2 = "p n g w j -> p (n g w j)"
            for hh in range(4):
                products(c, hh)
            codes[(nx, 0)] = quant(u0[:].rearrange(flat1), 1)[0]
            if v_next:
                ilv_pass("V", u23[:, 0, :, :], nx, 2, 4 * GCOLS, CH)
            else:
                ilv_head("V", u23[:, 0, :, :, :], nx, 2, GCOLS, DH)
            codes[(nx, 1)] = quant(u1[:].rearrange(flat1), 1)[0]
            codes[(nx, 2)], codes[(nx, 3)] = quant(u23[:].rearrange(flat2), 2)
            for hh in range(4):
                turn(c, hh)
            if v_next:
                for t in range(NT):
                    av = psa.tile([P, NKV * DH], F32, tag="acc", name="accv")
                    accv.append(av)
                order = [(g, t) for g in (0, 1) for t in range(NT)] + [(g, t) for t in range(NT) for g in (2, 3)]
                for g, t in order:
                    wc, ws = codes[(nx, g)]
                    blk = slice(t * P, (t + 1) * P)
                    nc.tensor.matmul_mx(
                        out=accv[t][:],
                        lhsT=xc[:, g, blk].bitcast(E5),
                        lhsT_scale=xs[:, g, blk],
                        rhs=wc.bitcast(E5),
                        rhs_scale=ws,
                        start=(g == 0),
                        stop=(g == G - 1),
                    )
            else:
                for hh in range(4):
                    mx(nx, hh)
            for hh in range(4):
                leave(c, hh)

        vdst = out_2[0].rearrange("h (p t) d -> t p h d", t=NT)
        for t in range(NT):
            o = opool.tile([P, NKV * DH], F32, tag="o", name="o")
            nc.vector.tensor_tensor(out=o[:], in0=accv[t][:], in1=bvb[:], op=ALU.add)
            queue = nc.sync if t % 2 == 0 else nc.scalar
            queue.dma_start(out=vdst[t], in_=o[:].rearrange("p (h d) -> p h d", h=NKV))
